import numpy as np
import ml_dtypes


def mxq(x, axis, fmt="e4m3"):
    dtype, down = {"e4m3": (ml_dtypes.float8_e4m3fn, 7), "e5m2": (ml_dtypes.float8_e5m2, 14)}[fmt]
    v = np.moveaxis(np.asarray(x, np.float32).astype(ml_dtypes.bfloat16).astype(np.float64), axis, -1)
    blocks = v.reshape(v.shape[:-1] + (-1, 32))
    amax = np.abs(blocks).max(-1, keepdims=True)
    byte = np.maximum(np.where(amax > 0, np.frexp(amax)[1] - 1 + 127, 0) - down, 1)
    scale = np.exp2(byte - 127.0)
    codes = (blocks / scale).astype(np.float32).astype(dtype).astype(np.float64)
    return np.moveaxis((codes * scale).reshape(v.shape), -1, axis)


WIDE = False


def mx_kscale(k):
    if not WIDE:
        return np.ones(k)
    levels = np.array([10, -10, 5, -5, 0])
    if k % 512:
        return np.exp2(np.random.permutation(np.resize(levels, k // 32))).repeat(32)
    a = np.empty((k // 512, 16))
    for p in range(k // 512):
        a[p, :8] = np.random.permutation(np.resize(levels, 8))
        for g in range(8):
            far = levels[np.abs(levels - a[p, g]) >= 10]
            a[p, g + 8] = far[np.random.randint(len(far))]
    return np.exp2(a.ravel()).repeat(32)


BF16 = ml_dtypes.bfloat16


def bf(x):
    return np.asarray(x, np.float32).astype(BF16)


def f64(x):
    return np.asarray(x).astype(np.float64)


B, DD, DK, CI, CO, L, NLC, PAD, KL = 1, 2, 2, 512, 128, 256, 4, 4, 9


def seg_lengths():
    cover = (L + PAD + PAD) // NLC - PAD - PAD
    lens = [cover] * NLC
    lens[-1] = L - cover * (NLC - 1)
    return lens


def setup_inputs():
    s = mx_kscale(CI)
    x = np.random.standard_normal((B, DD, DK, CI, L)) * s[:, None]
    weight = np.random.standard_normal((DD, DK, CO, CI, NLC, KL)) / np.sqrt(CI * KL) / s[:, None, None]
    bias = np.random.standard_normal((DD, DK, CO, NLC)) * 0.5
    return {"x": bf(x), "weight": bf(weight[..., None, :]), "conv_bias_param": bf(bias[..., None])}


def core(x, weight, conv_bias_param):
    xq = mxq(f64(x), 3, "e4m3")
    wq = mxq(f64(weight), 3, "e4m3")
    bias = f64(conv_bias_param)
    outs, start = [], 0
    for i, ln in enumerate(seg_lengths()):
        acc = np.zeros((B, DD, DK, CO, ln))
        for f in range(KL):
            lo = max(start, PAD - f)
            hi = min(start + ln, L + PAD - f)
            xs = xq[..., lo + f - PAD:hi + f - PAD].swapaxes(-1, -2)
            wf = wq[:, :, :, :, i, 0, f].swapaxes(-1, -2)
            acc[..., lo - start:hi - start] += (xs @ wf).swapaxes(-1, -2)
        outs.append(acc + bias[None, :, :, :, i, :])
        start += ln
    return np.concatenate(outs, axis=-1)


def e4m3fn_bytes(y):
    return np.clip(np.asarray(y, np.float64), -448.0, 448.0).astype(np.float32).astype(ml_dtypes.float8_e4m3fn).view(np.uint8)


def reference(x, weight, conv_bias_param):
    out = core(x, weight, conv_bias_param)
    s = np.max(np.abs(out), axis=-1, keepdims=True) / 448.0
    return out, e4m3fn_bytes(out / s)

@@ -1,0 +1,213 @@
+from contextlib import ExitStack
+
+import concourse.mybir as mybir
+from concourse.masks import make_identity
+
+F32 = mybir.dt.float32
+BF16 = mybir.dt.bfloat16
+I32 = mybir.dt.int32
+U8 = mybir.dt.uint8
+FP8X4 = mybir.dt.float8_e4m3fn_x4
+FP8 = mybir.dt.float8_e4m3fn
+ALU = mybir.AluOpType
+ACT = mybir.ActivationFunctionType
+AX = mybir.AxisListType
+
+P = 128
+G = 4
+CO = 128
+CI = 512
+NSEG = 4
+KL = 9
+NQ = NSEG * KL
+L = 256
+PAD = 4
+SEG_START = (0, 58, 116, 174)
+SEG_END = (58, 116, 174, 256)
+ROW = CI * NQ
+QC = 4
+CPG = NQ // QC
+NCYC = G * CPG
+LAGC = 3
+NWARM = 10
+NDUMMY = 0
+
+FLOPS = 2 * G * CO * CI * KL * L
+
+
+def tile_partiallyunsharedconv1d_pa_kernel(tc, x, weight, conv_bias_param, out_0, out_1):
+    nc = tc.nc
+    x_v = x.rearrange("b d k (p j) l -> p (b d k) j l", j=4)
+    w_v = weight.rearrange("d k o i s u f -> (d k) o (i s u f)")
+    b_v = conv_bias_param.rearrange("d k o s u -> o (d k) (s u)")
+    o0_v = out_0.rearrange("b d k o l -> (b d k) o l")
+    o1_v = out_1.rearrange("b d k o l -> (b d k) o l")
+
+    with ExitStack() as ctx:
+        const = ctx.enter_context(tc.tile_pool(name="const", bufs=1))
+        wpool = ctx.enter_context(tc.tile_pool(name="wraw", bufs=3))
+        gpool = ctx.enter_context(tc.tile_pool(name="grouped", bufs=4))
+        cpool = ctx.enter_context(tc.tile_pool(name="codes", bufs=LAGC + 3))
+        opool = ctx.enter_context(tc.tile_pool(name="outs", bufs=2))
+        tpool = ctx.enter_context(tc.psum_pool(name="tp", bufs=4))
+        apool = ctx.enter_context(tc.psum_pool(name="acc", bufs=3))
+        spool = ctx.enter_context(tc.psum_pool(name="scr", bufs=1))
+
+        xraw = const.tile([P, G, 4, L], BF16)
+        nc.sync.dma_start(out=xraw[:], in_=x_v)
+        biasb = const.tile([P, G, NSEG], BF16)
+        nc.scalar.dma_start(out=biasb[:], in_=b_v)
+
+        wtiles = {}
+
+        def load_w(g):
+            wsb = wpool.tile([P, ROW], BF16, name="wsb")
+            step = ROW // 4
+            for c in range(4):
+                nc.sync.dma_start(out=wsb[:, c * step:(c + 1) * step], in_=w_v[g, :, c * step:(c + 1) * step])
+            wtiles[g] = wsb
+
+        for g in range(3):
+            load_w(g)
+
+        ident = const.tile([P, P], F32)
+        make_identity(nc, ident[:])
+
+        biasf = const.tile([P, G, NSEG], F32)
+        nc.vector.tensor_copy(out=biasf[:], in_=biasb[:])
+
+        xg = const.tile([P, G, L, 4], BF16, align_bytes=64)
+        xsh = const.tile([P, KL, G, L], I32, align_bytes=64)
+        xss = const.tile([P, KL, L], U8, align_bytes=64)
+        nc.vector.memset(xss[:].bitcast(I32), 0)
+        nc.vector.memset(xsh[:, :, :, 0:PAD], 0)
+        nc.vector.memset(xsh[:, :, :, L - PAD:L], 0)
+        for g in range(G):
+            src = xraw[:, g].rearrange("p j l -> p l j")
+            if g % 2 == 0:
+                nc.vector.tensor_copy(out=xg[:, g], in_=src)
+            else:
+                nc.scalar.copy(out=xg[:, g], in_=src)
+        for g in range(G):
+            nc.vector.quantize_mx(
+                out=xsh[:, PAD, g, :].bitcast(FP8X4),
+                scales=xss[4 * g:P, PAD, :],
+                in_=xg[:, g].rearrange("p l j -> p (l j)"),
+            )
+        for f in range(KL):
+            d = f - PAD
+            if d == 0:
+                continue
+            lo = max(0, -d)
+            hi = min(L, L - d)
+            nc.vector.tensor_copy(out=xsh[:, f, :, lo:hi], in_=xsh[:, PAD, :, lo + d:hi + d])
+            nc.vector.tensor_copy(out=xss[:, f, lo:hi], in_=xss[:, PAD, lo + d:hi + d])
+
+        ctx.enter_context(tc.manual_schedule(engines={mybir.EngineType.PE}))
+        scr = spool.tile([P, 4 * P], F32, name="scr")
+
+        def dummy(count):
+            for i in range(count):
+                nc.tensor.matmul_mx(
+                    out=scr[:, 0:L],
+                    lhsT=xsh[:, PAD, 0, 0:P].bitcast(FP8X4),
+                    lhsT_scale=xss[0:P, PAD, 0:P],
+                    rhs=xsh[:, PAD, 0, :].bitcast(FP8X4),
+                    rhs_scale=xss[0:P, PAD, :],
+                    start=True,
+                    stop=True,
+                )
+
+        gate0 = 2 * (ROW // 4)
+        nc.tensor.matmul(scr[:, 2 * P:3 * P], lhsT=wtiles[0][:, gate0:gate0 + P], rhs=wtiles[0][:, gate0:gate0 + P], start=True, stop=True)
+        dummy(NWARM)
+
+        gro = {}
+        cod = {}
+        accs = {}
+
+        def quantise(c):
+            wc = cpool.tile([P, QC * CO], I32, name="wc", align_bytes=64)
+            ws = cpool.tile([P, QC * CO], U8, name="ws", align_bytes=64)
+            parts = 2 if c == NCYC - 1 else 1
+            wid = QC * CO // parts
+            for k in range(parts):
+                nc.vector.quantize_mx(
+                    out=wc[:, k * wid:(k + 1) * wid].bitcast(FP8X4),
+                    scales=ws[:, k * wid:(k + 1) * wid],
+                    in_=gro[c][:, 4 * k * wid:4 * (k + 1) * wid],
+                )
+            cod[c] = (wc, ws)
+
+        def epilogue(g):
+            res = opool.tile([P, L], F32, name="res")
+            for s in range(NSEG):
+                st, en = SEG_START[s], SEG_END[s]
+                base = (s % 2) * L
+                nc.scalar.activation(
+                    out=res[:, st:en],
+                    in_=accs[(g, s // 2)][:, base + st:base + en],
+                    func=ACT.Identity,
+                    bias=biasf[:, g, s:s + 1],
+                    scale=1.0,
+                )
+            nc.sync.dma_start(out=o0_v[g], in_=res[:])
+            amax = opool.tile([P, 1], F32, name="amax")
+            nc.vector.tensor_reduce(out=amax[:], in_=res[:], axis=AX.X, op=ALU.max, apply_absolute_value=True)
+            rcp = opool.tile([P, 1], F32, name="rcp")
+            nc.vector.reciprocal(out=rcp[:], in_=amax[:])
+            fac = opool.tile([P, 1], F32, name="fac")
+            nc.vector.tensor_scalar(out=fac[:], in0=rcp[:], scalar1=448.0, scalar2=None, op0=ALU.mult)
+            o8 = opool.tile([P, L], FP8, name="o8")
+            nc.vector.tensor_scalar(out=o8[:], in0=res[:], scalar1=fac[:, 0:1], scalar2=None, op0=ALU.mult, saturate=False)
+            nc.sync.dma_start(out=o1_v[g], in_=o8[:].bitcast(U8))
+
+        def multiply(c):
+            g, cc = divmod(c, CPG)
+            wc, ws = cod[c]
+            for ql in range(QC):
+                s, f = divmod(QC * cc + ql, KL)
+                if f == 0 and s % 2 == 0:
+                    acc = apool.tile([P, 2 * L], F32, name="acc")
+                    accs[(g, s // 2)] = acc
+                base = (s % 2) * L
+                nc.tensor.matmul_mx(
+                    out=accs[(g, s // 2)][:, base:base + L],
+                    lhsT=wc[:, ql * CO:(ql + 1) * CO].bitcast(FP8X4),
+                    lhsT_scale=ws[:, ql * CO:(ql + 1) * CO],
+                    rhs=xsh[:, f, g, :].bitcast(FP8X4),
+                    rhs_scale=xss[4 * g:P, f, :],
+                    start=(f == 0),
+                    stop=(f == KL - 1),
+                )
+            if cc == CPG - 1:
+                epilogue(g)
+
+        for c in range(NCYC):
+            g, cc = divmod(c, CPG)
+            wv = wtiles[g][:].bitcast(F32).rearrange("o (p t w) -> o t w p", t=4, w=NQ // 2)
+            grouped = gpool.tile([P, QC * CO * 4], BF16, name="grouped", align_bytes=64)
+            gro[c] = grouped
+            half = QC * CO * 2
+            for a in range(2):
+                tp = tpool.tile([P, 4 * P], F32, name="tp")
+                for t in range(4):
+                    nc.tensor.transpose(tp[:, t * P:(t + 1) * P], wv[:, t, 2 * cc + a, :], ident[:])
+                src = tp[:].bitcast(BF16).rearrange("p (t o e) -> p e o t", t=4, e=2)
+                dst = grouped[:, a * half:(a + 1) * half].rearrange("p (e o t) -> p e o t", e=2, t=4)
+                if a == 0 or (c % 3 == 2 and c != NCYC - 1):
+                    nc.scalar.copy(out=dst, in_=src)
+                else:
+                    nc.vector.tensor_copy(out=dst, in_=src)
+            if c >= 1:
+                quantise(c - 1)
+            if c >= LAGC:
+                multiply(c - LAGC)
+                dummy(NDUMMY)
+            else:
+                dummy(QC + NDUMMY)
+            if cc == CPG - 1 and g + 3 < G:
+                load_w(g + 3)
+        quantise(NCYC - 1)
+        for c in range(NCYC - LAGC, NCYC):
+            multiply(c)

@@ -12,6 +12,7 @@ FP8 = mybir.dt.float8_e4m3fn
 ALU = mybir.AluOpType
 ACT = mybir.ActivationFunctionType
 AX = mybir.AxisListType
+ENG = mybir.EngineType
 
 P = 128
 G = 4
@@ -24,13 +25,22 @@ L = 256
 PAD = 4
 SEG_START = (0, 58, 116, 174)
 SEG_END = (58, 116, 174, 256)
+SEG_WIN = (0, 0, 64, 128)
 ROW = CI * NQ
 QC = 4
 CPG = NQ // QC
+NT = 3
+DG = 3
+NCN = NT * CPG
 NCYC = G * CPG
 LAGC = 3
 NWARM = 10
-NDUMMY = 0
+OC = 32
+NCH = CO // OC
+DSTART = (5, 11, 20, 22)
+DRATE = (3, 3, 5, 3)
+DSTEP = (2, 2, 1, 1)
+DQRATE = 3
 
 FLOPS = 2 * G * CO * CI * KL * L
 
@@ -39,19 +49,21 @@ def tile_partiallyunsharedconv1d_pa_kernel(tc, x, weight, conv_bias_param, out_0
     nc = tc.nc
     x_v = x.rearrange("b d k (p j) l -> p (b d k) j l", j=4)
     w_v = weight.rearrange("d k o i s u f -> (d k) o (i s u f)")
+    wd_v = weight.rearrange("d k o (p t) s u f -> (d k) p o (t s u f)", t=4)
     b_v = conv_bias_param.rearrange("d k o s u -> o (d k) (s u)")
     o0_v = out_0.rearrange("b d k o l -> (b d k) o l")
     o1_v = out_1.rearrange("b d k o l -> (b d k) o l")
 
     with ExitStack() as ctx:
         const = ctx.enter_context(tc.tile_pool(name="const", bufs=1))
-        wpool = ctx.enter_context(tc.tile_pool(name="wraw", bufs=3))
+        wpool = ctx.enter_context(tc.tile_pool(name="wraw", bufs=2))
+        dpool = ctx.enter_context(tc.tile_pool(name="draw", bufs=2))
+        dgpool = ctx.enter_context(tc.tile_pool(name="dgrouped", bufs=CPG))
         gpool = ctx.enter_context(tc.tile_pool(name="grouped", bufs=4))
-        cpool = ctx.enter_context(tc.tile_pool(name="codes", bufs=LAGC + 3))
+        cpool = ctx.enter_context(tc.tile_pool(name="codes", bufs=LAGC + 7))
         opool = ctx.enter_context(tc.tile_pool(name="outs", bufs=2))
         tpool = ctx.enter_context(tc.psum_pool(name="tp", bufs=4))
-        apool = ctx.enter_context(tc.psum_pool(name="acc", bufs=3))
-        spool = ctx.enter_context(tc.psum_pool(name="scr", bufs=1))
+        apool = ctx.enter_context(tc.psum_pool(name="acc", bufs=4))
 
         xraw = const.tile([P, G, 4, L], BF16)
         nc.sync.dma_start(out=xraw[:], in_=x_v)
@@ -59,6 +71,7 @@ def tile_partiallyunsharedconv1d_pa_kernel(tc, x, weight, conv_bias_param, out_0
         nc.scalar.dma_start(out=biasb[:], in_=b_v)
 
         wtiles = {}
+        dtiles = {}
 
         def load_w(g):
             wsb = wpool.tile([P, ROW], BF16, name="wsb")
@@ -67,8 +80,15 @@ def tile_partiallyunsharedconv1d_pa_kernel(tc, x, weight, conv_bias_param, out_0
                 nc.sync.dma_start(out=wsb[:, c * step:(c + 1) * step], in_=w_v[g, :, c * step:(c + 1) * step])
             wtiles[g] = wsb
 
-        for g in range(3):
-            load_w(g)
+        def load_d(k):
+            dch = dpool.tile([P, OC, 4 * NQ], BF16, name="dch")
+            nc.sync.dma_start(out=dch[:], in_=wd_v[DG, :, k * OC:(k + 1) * OC, :])
+            dtiles[k] = dch
+
+        load_w(0)
+        load_d(0)
+        load_w(1)
+        load_d(1)
 
         ident = const.tile([P, P], F32)
         make_identity(nc, ident[:])
@@ -103,8 +123,8 @@ def tile_partiallyunsharedconv1d_pa_kernel(tc, x, weight, conv_bias_param, out_0
             nc.vector.tensor_copy(out=xsh[:, f, :, lo:hi], in_=xsh[:, PAD, :, lo + d:hi + d])
             nc.vector.tensor_copy(out=xss[:, f, lo:hi], in_=xss[:, PAD, lo + d:hi + d])
 
-        ctx.enter_context(tc.manual_schedule(engines={mybir.EngineType.PE}))
-        scr = spool.tile([P, 4 * P], F32, name="scr")
+        ctx.enter_context(tc.manual_schedule(engines={ENG.PE, ENG.DVE, ENG.Activation}))
+        scr = apool.tile([P, 4 * P], F32, name="acc")
 
         def dummy(count):
             for i in range(count):
@@ -125,11 +145,23 @@ def tile_partiallyunsharedconv1d_pa_kernel(tc, x, weight, conv_bias_param, out_0
         gro = {}
         cod = {}
         accs = {}
+        ress = {}
 
-        def quantise(c):
+        for j in range(CPG):
+            dgr = dgpool.tile([P, QC * CO * 4], BF16, name="dgr", align_bytes=64)
+            gro[NCN + j] = dgr
+
+        def regroup(k, j):
+            src = dtiles[k][:].rearrange("p o (t q) -> p o t q", t=4)[:, :, :, QC * j:QC * (j + 1)]
+            dst = gro[NCN + j][:].rearrange("p (q o t) -> p o t q", q=QC, t=4)[:, k * OC:(k + 1) * OC, :, :]
+            if k >= 2 and j % 4 == 3:
+                nc.scalar.copy(out=dst, in_=src)
+            else:
+                nc.vector.tensor_copy(out=dst, in_=src)
+
+        def quantise(c, parts):
             wc = cpool.tile([P, QC * CO], I32, name="wc", align_bytes=64)
             ws = cpool.tile([P, QC * CO], U8, name="ws", align_bytes=64)
-            parts = 2 if c == NCYC - 1 else 1
             wid = QC * CO // parts
             for k in range(parts):
                 nc.vector.quantize_mx(
@@ -139,19 +171,29 @@ def tile_partiallyunsharedconv1d_pa_kernel(tc, x, weight, conv_bias_param, out_0
                 )
             cod[c] = (wc, ws)
 
-        def epilogue(g):
+        def acc_slice(g, s, lo, hi):
+            if g == DG:
+                base = s * P - SEG_WIN[s]
+                return accs[(g, 0)][:, base + lo:base + hi]
+            base = (s % 2) * L
+            return accs[(g, s // 2)][:, base + lo:base + hi]
+
+        def epilogue_scalar(g):
             res = opool.tile([P, L], F32, name="res")
             for s in range(NSEG):
                 st, en = SEG_START[s], SEG_END[s]
-                base = (s % 2) * L
                 nc.scalar.activation(
                     out=res[:, st:en],
-                    in_=accs[(g, s // 2)][:, base + st:base + en],
+                    in_=acc_slice(g, s, st, en),
                     func=ACT.Identity,
                     bias=biasf[:, g, s:s + 1],
                     scale=1.0,
                 )
             nc.sync.dma_start(out=o0_v[g], in_=res[:])
+            ress[g] = res
+
+        def epilogue_vector(g):
+            res = ress[g]
             amax = opool.tile([P, 1], F32, name="amax")
             nc.vector.tensor_reduce(out=amax[:], in_=res[:], axis=AX.X, op=ALU.max, apply_absolute_value=True)
             rcp = opool.tile([P, 1], F32, name="rcp")
@@ -167,47 +209,79 @@ def tile_partiallyunsharedconv1d_pa_kernel(tc, x, weight, conv_bias_param, out_0
             wc, ws = cod[c]
             for ql in range(QC):
                 s, f = divmod(QC * cc + ql, KL)
-                if f == 0 and s % 2 == 0:
-                    acc = apool.tile([P, 2 * L], F32, name="acc")
-                    accs[(g, s // 2)] = acc
-                base = (s % 2) * L
+                if g == DG:
+                    if f == 0 and s == 0:
+                        acc = apool.tile([P, 4 * P], F32, name="acc")
+                        accs[(g, 0)] = acc
+                    lo, hi = SEG_WIN[s], SEG_WIN[s] + P
+                else:
+                    if f == 0 and s % 2 == 0:
+                        acc = apool.tile([P, 4 * P], F32, name="acc")
+                        accs[(g, s // 2)] = acc
+                    lo, hi = 0, L
                 nc.tensor.matmul_mx(
-                    out=accs[(g, s // 2)][:, base:base + L],
+                    out=acc_slice(g, s, lo, hi),
                     lhsT=wc[:, ql * CO:(ql + 1) * CO].bitcast(FP8X4),
                     lhsT_scale=ws[:, ql * CO:(ql + 1) * CO],
-                    rhs=xsh[:, f, g, :].bitcast(FP8X4),
-                    rhs_scale=xss[4 * g:P, f, :],
+                    rhs=xsh[:, f, g, lo:hi].bitcast(FP8X4),
+                    rhs_scale=xss[4 * g:P, f, lo:hi],
                     start=(f == 0),
                     stop=(f == KL - 1),
                 )
-            if cc == CPG - 1:
-                epilogue(g)
 
-        for c in range(NCYC):
-            g, cc = divmod(c, CPG)
-            wv = wtiles[g][:].bitcast(F32).rearrange("o (p t w) -> o t w p", t=4, w=NQ // 2)
-            grouped = gpool.tile([P, QC * CO * 4], BF16, name="grouped", align_bytes=64)
-            gro[c] = grouped
-            half = QC * CO * 2
-            for a in range(2):
-                tp = tpool.tile([P, 4 * P], F32, name="tp")
-                for t in range(4):
-                    nc.tensor.transpose(tp[:, t * P:(t + 1) * P], wv[:, t, 2 * cc + a, :], ident[:])
-                src = tp[:].bitcast(BF16).rearrange("p (t o e) -> p e o t", t=4, e=2)
-                dst = grouped[:, a * half:(a + 1) * half].rearrange("p (e o t) -> p e o t", e=2, t=4)
-                if a == 0 or (c % 3 == 2 and c != NCYC - 1):
-                    nc.scalar.copy(out=dst, in_=src)
-                else:
-                    nc.vector.tensor_copy(out=dst, in_=src)
-            if c >= 1:
-                quantise(c - 1)
-            if c >= LAGC:
+        def piece_cycle(k, j):
+            return DSTART[k] + DSTEP[k] * (j // DRATE[k])
+
+        def dq_cycle(j):
+            return DSTART[NCH - 1] + 1 + j // DQRATE
+
+        def busy_with_chunks(c):
+            return c >= DSTART[2] or any([piece_cycle(k, j) == c for k in range(NCH) for j in range(CPG)])
+
+        for c in range(NCN + LAGC + 2):
+            if c < NCN:
+                g, cc = divmod(c, CPG)
+                wv = wtiles[g][:].bitcast(F32).rearrange("o (p t w) -> o t w p", t=4, w=NQ // 2)
+                grouped = gpool.tile([P, QC * CO * 4], BF16, name="grouped", align_bytes=64)
+                gro[c] = grouped
+                half = QC * CO * 2
+                for a in range(2):
+                    tp = tpool.tile([P, 4 * P], F32, name="tp")
+                    for t in range(4):
+                        nc.tensor.transpose(tp[:, t * P:(t + 1) * P], wv[:, t, 2 * cc + a, :], ident[:])
+                    src = tp[:].bitcast(BF16).rearrange("p (t o e) -> p e o t", t=4, e=2)
+                    dst = grouped[:, a * half:(a + 1) * half].rearrange("p (e o t) -> p e o t", e=2, t=4)
+                    if a == 0 or busy_with_chunks(c):
+                        nc.scalar.copy(out=dst, in_=src)
+                    else:
+                        nc.vector.tensor_copy(out=dst, in_=src)
+            if 1 <= c <= NCN:
+                quantise(c - 1, 2 if c == NCN else 1)
+            for k in range(NCH):
+                for j in range(CPG):
+                    if piece_cycle(k, j) == c:
+                        regroup(k, j)
+            for j in range(CPG):
+                if dq_cycle(j) == c:
+                    quantise(NCN + j, 1)
+            for g in range(NT):
+                if c == (g + 1) * CPG + LAGC:
+                    epilogue_vector(g)
+            if c == dq_cycle(CPG - 1) + 2:
+                epilogue_vector(DG)
+            if c < LAGC:
+                dummy(QC)
+            elif c < NCN + LAGC:
                 multiply(c - LAGC)
-                dummy(NDUMMY)
-            else:
-                dummy(QC + NDUMMY)
-            if cc == CPG - 1 and g + 3 < G:
-                load_w(g + 3)
-        quantise(NCYC - 1)
-        for c in range(NCYC - LAGC, NCYC):
-            multiply(c)
+                if (c - LAGC) % CPG == CPG - 1:
+                    epilogue_scalar((c - LAGC) // CPG)
+            for j in range(CPG):
+                if dq_cycle(j) + 1 == c:
+                    multiply(NCN + j)
+            if c == dq_cycle(CPG - 1) + 1:
+                epilogue_scalar(DG)
+            if c == piece_cycle(0, CPG - 1):
+                load_w(2)
+                load_d(2)
+            if c == piece_cycle(1, CPG - 1):
+                load_d(3)

@@ -146,6 +146,7 @@ def tile_partiallyunsharedconv1d_pa_kernel(tc, x, weight, conv_bias_param, out_0
         cod = {}
         accs = {}
         ress = {}
+        small = {}
 
         for j in range(CPG):
             dgr = dgpool.tile([P, QC * CO * 4], BF16, name="dgr", align_bytes=64)
@@ -158,6 +159,7 @@ def tile_partiallyunsharedconv1d_pa_kernel(tc, x, weight, conv_bias_param, out_0
                 nc.scalar.copy(out=dst, in_=src)
             else:
                 nc.vector.tensor_copy(out=dst, in_=src)
+                one_step()
 
         def quantise(c, parts):
             wc = cpool.tile([P, QC * CO], I32, name="wc", align_bytes=64)
@@ -169,6 +171,7 @@ def tile_partiallyunsharedconv1d_pa_kernel(tc, x, weight, conv_bias_param, out_0
                     scales=ws[:, k * wid:(k + 1) * wid],
                     in_=gro[c][:, 4 * k * wid:4 * (k + 1) * wid],
                 )
+                one_step()
             cod[c] = (wc, ws)
 
         def acc_slice(g, s, lo, hi):
@@ -192,17 +195,33 @@ def tile_partiallyunsharedconv1d_pa_kernel(tc, x, weight, conv_bias_param, out_0
             nc.sync.dma_start(out=o0_v[g], in_=res[:])
             ress[g] = res
 
+        steps = []
+        done = {"n": 0}
+
         def epilogue_vector(g):
-            res = ress[g]
-            amax = opool.tile([P, 1], F32, name="amax")
-            nc.vector.tensor_reduce(out=amax[:], in_=res[:], axis=AX.X, op=ALU.max, apply_absolute_value=True)
-            rcp = opool.tile([P, 1], F32, name="rcp")
-            nc.vector.reciprocal(out=rcp[:], in_=amax[:])
-            fac = opool.tile([P, 1], F32, name="fac")
-            nc.vector.tensor_scalar(out=fac[:], in0=rcp[:], scalar1=448.0, scalar2=None, op0=ALU.mult)
-            o8 = opool.tile([P, L], FP8, name="o8")
-            nc.vector.tensor_scalar(out=o8[:], in0=res[:], scalar1=fac[:, 0:1], scalar2=None, op0=ALU.mult, saturate=False)
-            nc.sync.dma_start(out=o1_v[g], in_=o8[:].bitcast(U8))
+            steps.extend([(g, i) for i in range(4)])
+
+        def one_step():
+            if done["n"] == len(steps):
+                return
+            g, i = steps[done["n"]]
+            done["n"] = done["n"] + 1
+            if i == 0:
+                amax = opool.tile([P, 1], F32, name="amax")
+                nc.vector.tensor_reduce(out=amax[:], in_=ress[g][:], axis=AX.X, op=ALU.max, apply_absolute_value=True)
+                small[(g, 0)] = amax
+            elif i == 1:
+                rcp = opool.tile([P, 1], F32, name="rcp")
+                nc.vector.reciprocal(out=rcp[:], in_=small[(g, 0)][:])
+                small[(g, 1)] = rcp
+            elif i == 2:
+                fac = opool.tile([P, 1], F32, name="fac")
+                nc.vector.tensor_scalar(out=fac[:], in0=small[(g, 1)][:], scalar1=448.0, scalar2=None, op0=ALU.mult)
+                small[(g, 2)] = fac
+            else:
+                o8 = opool.tile([P, L], FP8, name="o8")
+                nc.vector.tensor_scalar(out=o8[:], in0=ress[g][:], scalar1=small[(g, 2)][:, 0:1], scalar2=None, op0=ALU.mult, saturate=False)
+                nc.sync.dma_start(out=o1_v[g], in_=o8[:].bitcast(U8))
 
         def multiply(c):
             g, cc = divmod(c, CPG)
@@ -255,6 +274,7 @@ def tile_partiallyunsharedconv1d_pa_kernel(tc, x, weight, conv_bias_param, out_0
                         nc.scalar.copy(out=dst, in_=src)
                     else:
                         nc.vector.tensor_copy(out=dst, in_=src)
+                        one_step()
             if 1 <= c <= NCN:
                 quantise(c - 1, 2 if c == NCN else 1)
             for k in range(NCH):
@@ -285,3 +305,5 @@ def tile_partiallyunsharedconv1d_pa_kernel(tc, x, weight, conv_bias_param, out_0
                 load_d(2)
             if c == piece_cycle(1, CPG - 1):
                 load_d(3)
+        for i in range(len(steps) - done["n"]):
+            one_step()

@@ -38,7 +38,8 @@ NWARM = 10
 OC = 32
 NCH = CO // OC
 DSTART = (5, 11, 20, 22)
-DRATE = (3, 3, 5, 3)
+NPC = 5
+DRATE = (2, 2, 3, 2)
 DSTEP = (2, 2, 1, 1)
 DQRATE = 3
 
@@ -58,7 +59,6 @@ def tile_partiallyunsharedconv1d_pa_kernel(tc, x, weight, conv_bias_param, out_0
         const = ctx.enter_context(tc.tile_pool(name="const", bufs=1))
         wpool = ctx.enter_context(tc.tile_pool(name="wraw", bufs=2))
         dpool = ctx.enter_context(tc.tile_pool(name="draw", bufs=2))
-        dgpool = ctx.enter_context(tc.tile_pool(name="dgrouped", bufs=CPG))
         gpool = ctx.enter_context(tc.tile_pool(name="grouped", bufs=4))
         cpool = ctx.enter_context(tc.tile_pool(name="codes", bufs=LAGC + 7))
         opool = ctx.enter_context(tc.tile_pool(name="outs", bufs=2))
@@ -148,18 +148,17 @@ def tile_partiallyunsharedconv1d_pa_kernel(tc, x, weight, conv_bias_param, out_0
         ress = {}
         small = {}
 
+        WID4 = QC * CO * 4
+        dall = const.tile([P, CPG * WID4], BF16, align_bytes=64)
         for j in range(CPG):
-            dgr = dgpool.tile([P, QC * CO * 4], BF16, name="dgr", align_bytes=64)
-            gro[NCN + j] = dgr
+            gro[NCN + j] = dall[:, j * WID4:(j + 1) * WID4]
 
-        def regroup(k, j):
-            src = dtiles[k][:].rearrange("p o (t q) -> p o t q", t=4)[:, :, :, QC * j:QC * (j + 1)]
-            dst = gro[NCN + j][:].rearrange("p (q o t) -> p o t q", q=QC, t=4)[:, k * OC:(k + 1) * OC, :, :]
-            if k >= 2 and j % 4 == 3:
-                nc.scalar.copy(out=dst, in_=src)
-            else:
-                nc.vector.tensor_copy(out=dst, in_=src)
-                one_step()
+        def regroup(k, u):
+            n = min(2, CPG - 2 * u)
+            src = dtiles[k][:].rearrange("p o (t j q) -> p j o t q", t=4, q=QC)[:, 2 * u:2 * u + n, :, :, :]
+            dst = dall[:].rearrange("p (j q o t) -> p j o t q", q=QC, o=CO, t=4)[:, 2 * u:2 * u + n, k * OC:(k + 1) * OC, :, :]
+            nc.vector.tensor_copy(out=dst, in_=src)
+            one_step()
 
         def quantise(c, parts):
             wc = cpool.tile([P, QC * CO], I32, name="wc", align_bytes=64)
@@ -248,14 +247,14 @@ def tile_partiallyunsharedconv1d_pa_kernel(tc, x, weight, conv_bias_param, out_0
                     stop=(f == KL - 1),
                 )
 
-        def piece_cycle(k, j):
-            return DSTART[k] + DSTEP[k] * (j // DRATE[k])
+        def piece_cycle(k, u):
+            return DSTART[k] + DSTEP[k] * (u // DRATE[k])
 
         def dq_cycle(j):
             return DSTART[NCH - 1] + 1 + j // DQRATE
 
         def busy_with_chunks(c):
-            return c >= DSTART[2] or any([piece_cycle(k, j) == c for k in range(NCH) for j in range(CPG)])
+            return c >= DSTART[2] or any([piece_cycle(k, u) == c for k in range(NCH) for u in range(NPC)])
 
         for c in range(NCN + LAGC + 2):
             if c < NCN:
@@ -278,9 +277,9 @@ def tile_partiallyunsharedconv1d_pa_kernel(tc, x, weight, conv_bias_param, out_0
             if 1 <= c <= NCN:
                 quantise(c - 1, 2 if c == NCN else 1)
             for k in range(NCH):
-                for j in range(CPG):
-                    if piece_cycle(k, j) == c:
-                        regroup(k, j)
+                for u in range(NPC):
+                    if piece_cycle(k, u) == c:
+                        regroup(k, u)
             for j in range(CPG):
                 if dq_cycle(j) == c:
                     quantise(NCN + j, 1)
@@ -300,10 +299,10 @@ def tile_partiallyunsharedconv1d_pa_kernel(tc, x, weight, conv_bias_param, out_0
                     multiply(NCN + j)
             if c == dq_cycle(CPG - 1) + 1:
                 epilogue_scalar(DG)
-            if c == piece_cycle(0, CPG - 1):
+            if c == piece_cycle(0, NPC - 1):
                 load_w(2)
                 load_d(2)
-            if c == piece_cycle(1, CPG - 1):
+            if c == piece_cycle(1, NPC - 1):
                 load_d(3)
         for i in range(len(steps) - done["n"]):
             one_step()

@@ -35,13 +35,18 @@ NCN = NT * CPG
 NCYC = G * CPG
 LAGC = 3
 NWARM = 10
-OC = 32
-NCH = CO // OC
+OCS = (24, 40, 32, 32)
+OFF = (0, 24, 64, 96)
+NCH = 4
 DSTART = (5, 11, 20, 22)
-NPC = 5
-DRATE = (2, 2, 3, 2)
+NPC = 3
+DRATE = (1, 1, 2, 1)
 DSTEP = (2, 2, 1, 1)
 DQRATE = 3
+DLAG = 2
+SCAST = 1
+PRE0 = 5
+NPRE = CPG - PRE0
 
 FLOPS = 2 * G * CO * CI * KL * L
 
@@ -60,12 +65,13 @@ def tile_partiallyunsharedconv1d_pa_kernel(tc, x, weight, conv_bias_param, out_0
         wpool = ctx.enter_context(tc.tile_pool(name="wraw", bufs=2))
         dpool = ctx.enter_context(tc.tile_pool(name="draw", bufs=2))
         gpool = ctx.enter_context(tc.tile_pool(name="grouped", bufs=4))
-        cpool = ctx.enter_context(tc.tile_pool(name="codes", bufs=LAGC + 7))
+        cpool = ctx.enter_context(tc.tile_pool(name="codes", bufs=LAGC + 9))
         opool = ctx.enter_context(tc.tile_pool(name="outs", bufs=2))
+        spool = ctx.enter_context(tc.tile_pool(name="stage", bufs=2))
         tpool = ctx.enter_context(tc.psum_pool(name="tp", bufs=4))
         apool = ctx.enter_context(tc.psum_pool(name="acc", bufs=4))
 
-        xraw = const.tile([P, G, 4, L], BF16)
+        xraw = spool.tile([P, G, 4, L], BF16, name="stage", align_bytes=64)
         nc.sync.dma_start(out=xraw[:], in_=x_v)
         biasb = const.tile([P, G, NSEG], BF16)
         nc.scalar.dma_start(out=biasb[:], in_=b_v)
@@ -81,8 +87,8 @@ def tile_partiallyunsharedconv1d_pa_kernel(tc, x, weight, conv_bias_param, out_0
             wtiles[g] = wsb
 
         def load_d(k):
-            dch = dpool.tile([P, OC, 4 * NQ], BF16, name="dch")
-            nc.sync.dma_start(out=dch[:], in_=wd_v[DG, :, k * OC:(k + 1) * OC, :])
+            dch = dpool.tile([P, max(OCS), 4 * NQ], BF16, name="dch")
+            nc.sync.dma_start(out=dch[:, 0:OCS[k], :], in_=wd_v[DG, :, OFF[k]:OFF[k] + OCS[k], :])
             dtiles[k] = dch
 
         load_w(0)
@@ -93,10 +99,12 @@ def tile_partiallyunsharedconv1d_pa_kernel(tc, x, weight, conv_bias_param, out_0
         ident = const.tile([P, P], F32)
         make_identity(nc, ident[:])
 
+        zero = const.tile([P, 1], F32)
+        nc.vector.memset(zero[:], 0.0)
         biasf = const.tile([P, G, NSEG], F32)
         nc.vector.tensor_copy(out=biasf[:], in_=biasb[:])
 
-        xg = const.tile([P, G, L, 4], BF16, align_bytes=64)
+        xg = spool.tile([P, G, L, 4], BF16, name="stage", align_bytes=64)
         xsh = const.tile([P, KL, G, L], I32, align_bytes=64)
         xss = const.tile([P, KL, L], U8, align_bytes=64)
         nc.vector.memset(xss[:].bitcast(I32), 0)
@@ -114,6 +122,22 @@ def tile_partiallyunsharedconv1d_pa_kernel(tc, x, weight, conv_bias_param, out_0
                 scales=xss[4 * g:P, PAD, :],
                 in_=xg[:, g].rearrange("p l j -> p (l j)"),
             )
+        pres = []
+        for h in range(NPRE // 2):
+            pre = spool.tile([P, 2 * QC * CI], BF16, name="stage", align_bytes=64)
+            pres.append(pre)
+
+        def pair(copy, c4, j):
+            step = ROW // 4
+            q0 = QC * (PRE0 + j)
+            src = wtiles[0][:, c4 * step:(c4 + 1) * step].rearrange("o (p u e q) -> o u p e q", u=2, e=2, q=NQ)[:, :, :, :, q0:q0 + QC]
+            dst = pres[j // 2][:].rearrange("o (j q u p e) -> o j u p e q", j=2, q=QC, u=2, e=2)[:, j % 2, :, 32 * c4:32 * c4 + 32, :, :]
+            copy(out=dst, in_=src)
+
+        for c4 in range(3):
+            for j in range(NPRE):
+                pair(nc.scalar.copy, c4, j)
+
         for f in range(KL):
             d = f - PAD
             if d == 0:
@@ -122,6 +146,8 @@ def tile_partiallyunsharedconv1d_pa_kernel(tc, x, weight, conv_bias_param, out_0
             hi = min(L, L - d)
             nc.vector.tensor_copy(out=xsh[:, f, :, lo:hi], in_=xsh[:, PAD, :, lo + d:hi + d])
             nc.vector.tensor_copy(out=xss[:, f, lo:hi], in_=xss[:, PAD, lo + d:hi + d])
+        for j in range(NPRE):
+            pair(nc.vector.tensor_copy, 3, j)
 
         ctx.enter_context(tc.manual_schedule(engines={ENG.PE, ENG.DVE, ENG.Activation}))
         scr = apool.tile([P, 4 * P], F32, name="acc")
@@ -154,11 +180,14 @@ def tile_partiallyunsharedconv1d_pa_kernel(tc, x, weight, conv_bias_param, out_0
             gro[NCN + j] = dall[:, j * WID4:(j + 1) * WID4]
 
         def regroup(k, u):
-            n = min(2, CPG - 2 * u)
-            src = dtiles[k][:].rearrange("p o (t j q) -> p j o t q", t=4, q=QC)[:, 2 * u:2 * u + n, :, :, :]
-            dst = dall[:].rearrange("p (j q o t) -> p j o t q", q=QC, o=CO, t=4)[:, 2 * u:2 * u + n, k * OC:(k + 1) * OC, :, :]
-            nc.vector.tensor_copy(out=dst, in_=src)
-            one_step()
+            n = min(4, CPG - 4 * u)
+            src = dtiles[k][:].rearrange("p o (t j q) -> p j o t q", t=4, q=QC)[:, 4 * u:4 * u + n, 0:OCS[k], :, :]
+            dst = dall[:].rearrange("p (j q o t) -> p j o t q", q=QC, o=CO, t=4)[:, 4 * u:4 * u + n, OFF[k]:OFF[k] + OCS[k], :, :]
+            if k == NCH - 1 and u == NPC - 1:
+                nc.scalar.copy(out=dst, in_=src)
+            else:
+                nc.vector.tensor_copy(out=dst, in_=src)
+                one_step()
 
         def quantise(c, parts):
             wc = cpool.tile([P, QC * CO], I32, name="wc", align_bytes=64)
@@ -213,6 +242,9 @@ def tile_partiallyunsharedconv1d_pa_kernel(tc, x, weight, conv_bias_param, out_0
                 rcp = opool.tile([P, 1], F32, name="rcp")
                 nc.vector.reciprocal(out=rcp[:], in_=small[(g, 0)][:])
                 small[(g, 1)] = rcp
+                if g == SCAST:
+                    ssteps.extend([(g, 2, now["c"] + 2), (g, 3, now["c"] + 2)])
+                    done["n"] = done["n"] + 2
             elif i == 2:
                 fac = opool.tile([P, 1], F32, name="fac")
                 nc.vector.tensor_scalar(out=fac[:], in0=small[(g, 1)][:], scalar1=448.0, scalar2=None, op0=ALU.mult)
@@ -220,6 +252,24 @@ def tile_partiallyunsharedconv1d_pa_kernel(tc, x, weight, conv_bias_param, out_0
             else:
                 o8 = opool.tile([P, L], FP8, name="o8")
                 nc.vector.tensor_scalar(out=o8[:], in0=ress[g][:], scalar1=small[(g, 2)][:, 0:1], scalar2=None, op0=ALU.mult, saturate=False)
+                nc.sync.dma_start(out=o1_v[g], in_=o8[:].bitcast(U8))
+
+        ssteps = []
+        sdone = {"n": 0}
+        now = {"c": 0}
+
+        def one_scalar_step():
+            if sdone["n"] == len(ssteps) or ssteps[sdone["n"]][2] > now["c"]:
+                return
+            g, i, first = ssteps[sdone["n"]]
+            sdone["n"] = sdone["n"] + 1
+            if i == 2:
+                fac = opool.tile([P, 1], F32, name="fac")
+                nc.scalar.activation(out=fac[:], in_=small[(g, 1)][:], func=ACT.Identity, scale=448.0)
+                small[(g, 2)] = fac
+            else:
+                o8 = opool.tile([P, L], FP8, name="o8")
+                nc.scalar.activation(out=o8[:], in_=ress[g][:], func=ACT.Identity, scale=small[(g, 2)][:, 0:1], bias=zero[:, 0:1], saturate=False)
                 nc.sync.dma_start(out=o1_v[g], in_=o8[:].bitcast(U8))
 
         def multiply(c):
@@ -257,6 +307,7 @@ def tile_partiallyunsharedconv1d_pa_kernel(tc, x, weight, conv_bias_param, out_0
             return c >= DSTART[2] or any([piece_cycle(k, u) == c for k in range(NCH) for u in range(NPC)])
 
         for c in range(NCN + LAGC + 2):
+            now["c"] = c
             if c < NCN:
                 g, cc = divmod(c, CPG)
                 wv = wtiles[g][:].bitcast(F32).rearrange("o (p t w) -> o t w p", t=4, w=NQ // 2)
@@ -265,12 +316,22 @@ def tile_partiallyunsharedconv1d_pa_kernel(tc, x, weight, conv_bias_param, out_0
                 half = QC * CO * 2
                 for a in range(2):
                     tp = tpool.tile([P, 4 * P], F32, name="tp")
-                    for t in range(4):
-                        nc.tensor.transpose(tp[:, t * P:(t + 1) * P], wv[:, t, 2 * cc + a, :], ident[:])
-                    src = tp[:].bitcast(BF16).rearrange("p (t o e) -> p e o t", t=4, e=2)
-                    dst = grouped[:, a * half:(a + 1) * half].rearrange("p (e o t) -> p e o t", e=2, t=4)
+                    if g == 0 and cc >= PRE0:
+                        j = cc - PRE0
+                        prw = pres[j // 2][:].bitcast(F32)
+                        for i in range(4):
+                            w0 = (((j % 2) * QC + 2 * a) * 2 + i) * P
+                            nc.tensor.transpose(tp[:, i * P:(i + 1) * P], prw[:, w0:w0 + P], ident[:])
+                        src = tp[:].rearrange("p (e u o) -> p e o u", e=2, u=2)
+                        dst = grouped[:, a * half:(a + 1) * half].bitcast(F32).rearrange("p (e o u) -> p e o u", e=2, u=2)
+                    else:
+                        for t in range(4):
+                            nc.tensor.transpose(tp[:, t * P:(t + 1) * P], wv[:, t, 2 * cc + a, :], ident[:])
+                        src = tp[:].bitcast(BF16).rearrange("p (t o e) -> p e o t", t=4, e=2)
+                        dst = grouped[:, a * half:(a + 1) * half].rearrange("p (e o t) -> p e o t", e=2, t=4)
                     if a == 0 or busy_with_chunks(c):
                         nc.scalar.copy(out=dst, in_=src)
+                        one_scalar_step()
                     else:
                         nc.vector.tensor_copy(out=dst, in_=src)
                         one_step()
@@ -286,7 +347,7 @@ def tile_partiallyunsharedconv1d_pa_kernel(tc, x, weight, conv_bias_param, out_0
             for g in range(NT):
                 if c == (g + 1) * CPG + LAGC:
                     epilogue_vector(g)
-            if c == dq_cycle(CPG - 1) + 2:
+            if c == dq_cycle(CPG - 1) + DLAG + 1:
                 epilogue_vector(DG)
             if c < LAGC:
                 dummy(QC)
@@ -295,9 +356,9 @@ def tile_partiallyunsharedconv1d_pa_kernel(tc, x, weight, conv_bias_param, out_0
                 if (c - LAGC) % CPG == CPG - 1:
                     epilogue_scalar((c - LAGC) // CPG)
             for j in range(CPG):
-                if dq_cycle(j) + 1 == c:
+                if dq_cycle(j) + DLAG == c:
                     multiply(NCN + j)
-            if c == dq_cycle(CPG - 1) + 1:
+            if c == dq_cycle(CPG - 1) + DLAG:
                 epilogue_scalar(DG)
             if c == piece_cycle(0, NPC - 1):
                 load_w(2)

@@ -45,8 +45,9 @@ DSTEP = (2, 2, 1, 1)
 DQRATE = 3
 DLAG = 2
 SCAST = 1
-PRE0 = 5
-NPRE = CPG - PRE0
+PRE0 = 3
+STG0 = 5
+VS0 = 0
 
 FLOPS = 2 * G * CO * CI * KL * L
 
@@ -72,7 +73,8 @@ def tile_partiallyunsharedconv1d_pa_kernel(tc, x, weight, conv_bias_param, out_0
         apool = ctx.enter_context(tc.psum_pool(name="acc", bufs=4))
 
         xraw = spool.tile([P, G, 4, L], BF16, name="stage", align_bytes=64)
-        nc.sync.dma_start(out=xraw[:], in_=x_v)
+        for g in range(G):
+            nc.sync.dma_start(out=xraw[:, g], in_=x_v[:, g])
         biasb = const.tile([P, G, NSEG], BF16)
         nc.scalar.dma_start(out=biasb[:], in_=b_v)
 
@@ -122,21 +124,29 @@ def tile_partiallyunsharedconv1d_pa_kernel(tc, x, weight, conv_bias_param, out_0
                 scales=xss[4 * g:P, PAD, :],
                 in_=xg[:, g].rearrange("p l j -> p (l j)"),
             )
+        WID4 = QC * CO * 4
+        dall = const.tile([P, CPG * WID4], BF16, align_bytes=64)
         pres = []
-        for h in range(NPRE // 2):
-            pre = spool.tile([P, 2 * QC * CI], BF16, name="stage", align_bytes=64)
+        for h in range((CPG - STG0) // 2):
+            pre = spool.tile([P, 2 * WID4], BF16, name="stage", align_bytes=64)
             pres.append(pre)
 
-        def pair(copy, c4, j):
+        def pre_ap(cc):
+            if cc >= STG0:
+                j = cc - STG0
+                return pres[j // 2][:, (j % 2) * WID4:(j % 2 + 1) * WID4]
+            return dall[:, (cc + 2) * WID4:(cc + 3) * WID4]
+
+        def pair(copy, c4, cc):
             step = ROW // 4
-            q0 = QC * (PRE0 + j)
+            q0 = QC * cc
             src = wtiles[0][:, c4 * step:(c4 + 1) * step].rearrange("o (p u e q) -> o u p e q", u=2, e=2, q=NQ)[:, :, :, :, q0:q0 + QC]
-            dst = pres[j // 2][:].rearrange("o (j q u p e) -> o j u p e q", j=2, q=QC, u=2, e=2)[:, j % 2, :, 32 * c4:32 * c4 + 32, :, :]
+            dst = pre_ap(cc).rearrange("o (q u p e) -> o u p e q", q=QC, u=2, e=2)[:, :, 32 * c4:32 * c4 + 32, :, :]
             copy(out=dst, in_=src)
 
         for c4 in range(3):
-            for j in range(NPRE):
-                pair(nc.scalar.copy, c4, j)
+            for cc in range(STG0, CPG):
+                pair(nc.scalar.copy, c4, cc)
 
         for f in range(KL):
             d = f - PAD
@@ -146,8 +156,11 @@ def tile_partiallyunsharedconv1d_pa_kernel(tc, x, weight, conv_bias_param, out_0
             hi = min(L, L - d)
             nc.vector.tensor_copy(out=xsh[:, f, :, lo:hi], in_=xsh[:, PAD, :, lo + d:hi + d])
             nc.vector.tensor_copy(out=xss[:, f, lo:hi], in_=xss[:, PAD, lo + d:hi + d])
-        for j in range(NPRE):
-            pair(nc.vector.tensor_copy, 3, j)
+        for c4 in range(3):
+            for cc in range(PRE0, STG0):
+                pair(nc.vector.tensor_copy, c4, cc)
+        for cc in range(PRE0, CPG):
+            pair(nc.vector.tensor_copy, 3, cc)
 
         ctx.enter_context(tc.manual_schedule(engines={ENG.PE, ENG.DVE, ENG.Activation}))
         scr = apool.tile([P, 4 * P], F32, name="acc")
@@ -174,8 +187,6 @@ def tile_partiallyunsharedconv1d_pa_kernel(tc, x, weight, conv_bias_param, out_0
         ress = {}
         small = {}
 
-        WID4 = QC * CO * 4
-        dall = const.tile([P, CPG * WID4], BF16, align_bytes=64)
         for j in range(CPG):
             gro[NCN + j] = dall[:, j * WID4:(j + 1) * WID4]
 
@@ -317,10 +328,9 @@ def tile_partiallyunsharedconv1d_pa_kernel(tc, x, weight, conv_bias_param, out_0
                 for a in range(2):
                     tp = tpool.tile([P, 4 * P], F32, name="tp")
                     if g == 0 and cc >= PRE0:
-                        j = cc - PRE0
-                        prw = pres[j // 2][:].bitcast(F32)
+                        prw = pre_ap(cc).bitcast(F32)
                         for i in range(4):
-                            w0 = (((j % 2) * QC + 2 * a) * 2 + i) * P
+                            w0 = (4 * a + i) * P
                             nc.tensor.transpose(tp[:, i * P:(i + 1) * P], prw[:, w0:w0 + P], ident[:])
                         src = tp[:].rearrange("p (e u o) -> p e o u", e=2, u=2)
                         dst = grouped[:, a * half:(a + 1) * half].bitcast(F32).rearrange("p (e o u) -> p e o u", e=2, u=2)
@@ -329,7 +339,7 @@ def tile_partiallyunsharedconv1d_pa_kernel(tc, x, weight, conv_bias_param, out_0
                             nc.tensor.transpose(tp[:, t * P:(t + 1) * P], wv[:, t, 2 * cc + a, :], ident[:])
                         src = tp[:].bitcast(BF16).rearrange("p (t o e) -> p e o t", t=4, e=2)
                         dst = grouped[:, a * half:(a + 1) * half].rearrange("p (e o t) -> p e o t", e=2, t=4)
-                    if a == 0 or busy_with_chunks(c):
+                    if a == 0 or c < VS0 or busy_with_chunks(c):
                         nc.scalar.copy(out=dst, in_=src)
                         one_scalar_step()
                     else:

@@ -39,6 +39,7 @@ OCS = (24, 40, 32, 32)
 OFF = (0, 24, 64, 96)
 NCH = 4
 DSTART = (5, 11, 20, 22)
+PC0 = (5, 8, 9)
 NPC = 3
 DRATE = (1, 1, 2, 1)
 DSTEP = (2, 2, 1, 1)
@@ -46,7 +47,9 @@ DQRATE = 3
 DLAG = 2
 SCAST = 1
 PRE0 = 3
-STG0 = 5
+SP0 = 5
+P1C0 = 5
+P1Q = (4, 6, 8, 10)
 VS0 = 0
 
 FLOPS = 2 * G * CO * CI * KL * L
@@ -69,8 +72,8 @@ def tile_partiallyunsharedconv1d_pa_kernel(tc, x, weight, conv_bias_param, out_0
         cpool = ctx.enter_context(tc.tile_pool(name="codes", bufs=LAGC + 9))
         opool = ctx.enter_context(tc.tile_pool(name="outs", bufs=2))
         spool = ctx.enter_context(tc.tile_pool(name="stage", bufs=2))
-        tpool = ctx.enter_context(tc.psum_pool(name="tp", bufs=4))
-        apool = ctx.enter_context(tc.psum_pool(name="acc", bufs=4))
+        tpool = ctx.enter_context(tc.psum_pool(name="tp", bufs=5))
+        apool = ctx.enter_context(tc.psum_pool(name="acc", bufs=3))
 
         xraw = spool.tile([P, G, 4, L], BF16, name="stage", align_bytes=64)
         for g in range(G):
@@ -127,15 +130,23 @@ def tile_partiallyunsharedconv1d_pa_kernel(tc, x, weight, conv_bias_param, out_0
         WID4 = QC * CO * 4
         dall = const.tile([P, CPG * WID4], BF16, align_bytes=64)
         pres = []
-        for h in range((CPG - STG0) // 2):
+        for h in range((CPG - P1C0) // 2):
             pre = spool.tile([P, 2 * WID4], BF16, name="stage", align_bytes=64)
             pres.append(pre)
 
         def pre_ap(cc):
-            if cc >= STG0:
-                j = cc - STG0
-                return pres[j // 2][:, (j % 2) * WID4:(j % 2 + 1) * WID4]
-            return dall[:, (cc + 2) * WID4:(cc + 3) * WID4]
+            return dall[:, cc * WID4:(cc + 1) * WID4]
+
+        def pre1_ap(cc):
+            j = cc - P1C0
+            return pres[j // 2][:, (j % 2) * WID4:(j % 2 + 1) * WID4]
+
+        def pair1(copy, c4, cc):
+            step = ROW // 4
+            q0 = QC * cc
+            src = wtiles[1][:, c4 * step:(c4 + 1) * step].rearrange("o (p u e q) -> o u p e q", u=2, e=2, q=NQ)[:, :, :, :, q0:q0 + QC]
+            dst = pre1_ap(cc).rearrange("o (q u p e) -> o u p e q", q=QC, u=2, e=2)[:, :, 32 * c4:32 * c4 + 32, :, :]
+            copy(out=dst, in_=src)
 
         def pair(copy, c4, cc):
             step = ROW // 4
@@ -145,7 +156,7 @@ def tile_partiallyunsharedconv1d_pa_kernel(tc, x, weight, conv_bias_param, out_0
             copy(out=dst, in_=src)
 
         for c4 in range(3):
-            for cc in range(STG0, CPG):
+            for cc in range(SP0, CPG):
                 pair(nc.scalar.copy, c4, cc)
 
         for f in range(KL):
@@ -157,7 +168,7 @@ def tile_partiallyunsharedconv1d_pa_kernel(tc, x, weight, conv_bias_param, out_0
             nc.vector.tensor_copy(out=xsh[:, f, :, lo:hi], in_=xsh[:, PAD, :, lo + d:hi + d])
             nc.vector.tensor_copy(out=xss[:, f, lo:hi], in_=xss[:, PAD, lo + d:hi + d])
         for c4 in range(3):
-            for cc in range(PRE0, STG0):
+            for cc in range(PRE0, SP0):
                 pair(nc.vector.tensor_copy, c4, cc)
         for cc in range(PRE0, CPG):
             pair(nc.vector.tensor_copy, 3, cc)
@@ -220,9 +231,12 @@ def tile_partiallyunsharedconv1d_pa_kernel(tc, x, weight, conv_bias_param, out_0
             base = (s % 2) * L
             return accs[(g, s // 2)][:, base + lo:base + hi]
 
-        def epilogue_scalar(g):
-            res = opool.tile([P, L], F32, name="res")
-            for s in range(NSEG):
+        def epilogue_scalar(g, segs):
+            if segs[0] == 0:
+                res = opool.tile([P, L], F32, name="res")
+                ress[g] = res
+            res = ress[g]
+            for s in segs:
                 st, en = SEG_START[s], SEG_END[s]
                 nc.scalar.activation(
                     out=res[:, st:en],
@@ -231,8 +245,8 @@ def tile_partiallyunsharedconv1d_pa_kernel(tc, x, weight, conv_bias_param, out_0
                     bias=biasf[:, g, s:s + 1],
                     scale=1.0,
                 )
-            nc.sync.dma_start(out=o0_v[g], in_=res[:])
-            ress[g] = res
+            if segs[-1] == NSEG - 1:
+                nc.sync.dma_start(out=o0_v[g], in_=res[:])
 
         steps = []
         done = {"n": 0}
@@ -309,7 +323,7 @@ def tile_partiallyunsharedconv1d_pa_kernel(tc, x, weight, conv_bias_param, out_0
                 )
 
         def piece_cycle(k, u):
-            return DSTART[k] + DSTEP[k] * (u // DRATE[k])
+            return PC0[u] if k == 0 else DSTART[k] + DSTEP[k] * (u // DRATE[k])
 
         def dq_cycle(j):
             return DSTART[NCH - 1] + 1 + j // DQRATE
@@ -327,8 +341,8 @@ def tile_partiallyunsharedconv1d_pa_kernel(tc, x, weight, conv_bias_param, out_0
                 half = QC * CO * 2
                 for a in range(2):
                     tp = tpool.tile([P, 4 * P], F32, name="tp")
-                    if g == 0 and cc >= PRE0:
-                        prw = pre_ap(cc).bitcast(F32)
+                    if (g == 0 and cc >= PRE0) or (g == 1 and cc >= P1C0):
+                        prw = (pre_ap(cc) if g == 0 else pre1_ap(cc)).bitcast(F32)
                         for i in range(4):
                             w0 = (4 * a + i) * P
                             nc.tensor.transpose(tp[:, i * P:(i + 1) * P], prw[:, w0:w0 + P], ident[:])
@@ -345,8 +359,17 @@ def tile_partiallyunsharedconv1d_pa_kernel(tc, x, weight, conv_bias_param, out_0
                     else:
                         nc.vector.tensor_copy(out=dst, in_=src)
                         one_step()
+            for c4 in range(4):
+                for k in range(CPG - P1C0):
+                    if P1Q[c4] + k // 2 == c and k % 2 == 0:
+                        pair1(nc.scalar.copy, c4, P1C0 + k)
             if 1 <= c <= NCN:
                 quantise(c - 1, 2 if c == NCN else 1)
+            for c4 in range(4):
+                for k in range(CPG - P1C0):
+                    if P1Q[c4] + k // 2 == c and k % 2 == 1:
+                        pair1(nc.vector.tensor_copy, c4, P1C0 + k)
+                        one_step()
             for k in range(NCH):
                 for u in range(NPC):
                     if piece_cycle(k, u) == c:
@@ -363,13 +386,15 @@ def tile_partiallyunsharedconv1d_pa_kernel(tc, x, weight, conv_bias_param, out_0
                 dummy(QC)
             elif c < NCN + LAGC:
                 multiply(c - LAGC)
+                if (c - LAGC) % CPG == CPG // 2:
+                    epilogue_scalar((c - LAGC) // CPG, (0, 1))
                 if (c - LAGC) % CPG == CPG - 1:
-                    epilogue_scalar((c - LAGC) // CPG)
+                    epilogue_scalar((c - LAGC) // CPG, (2, 3))
             for j in range(CPG):
                 if dq_cycle(j) + DLAG == c:
                     multiply(NCN + j)
             if c == dq_cycle(CPG - 1) + DLAG:
-                epilogue_scalar(DG)
+                epilogue_scalar(DG, (0, 1, 2, 3))
             if c == piece_cycle(0, NPC - 1):
                 load_w(2)
                 load_d(2)

@@ -45,11 +45,12 @@ DRATE = (1, 1, 2, 1)
 DSTEP = (2, 2, 1, 1)
 DQRATE = 3
 DLAG = 2
-SCAST = 1
+SCAST = (1, 3)
 PRE0 = 3
 SP0 = 5
 P1C0 = 5
 P1Q = (4, 6, 8, 10)
+NARROW0 = 22
 VS0 = 0
 
 FLOPS = 2 * G * CO * CI * KL * L
@@ -70,7 +71,7 @@ def tile_partiallyunsharedconv1d_pa_kernel(tc, x, weight, conv_bias_param, out_0
         dpool = ctx.enter_context(tc.tile_pool(name="draw", bufs=2))
         gpool = ctx.enter_context(tc.tile_pool(name="grouped", bufs=4))
         cpool = ctx.enter_context(tc.tile_pool(name="codes", bufs=LAGC + 9))
-        opool = ctx.enter_context(tc.tile_pool(name="outs", bufs=2))
+        opool = ctx.enter_context(tc.tile_pool(name="outs", bufs=3))
         spool = ctx.enter_context(tc.tile_pool(name="stage", bufs=2))
         tpool = ctx.enter_context(tc.psum_pool(name="tp", bufs=5))
         apool = ctx.enter_context(tc.psum_pool(name="acc", bufs=3))
@@ -267,8 +268,8 @@ def tile_partiallyunsharedconv1d_pa_kernel(tc, x, weight, conv_bias_param, out_0
                 rcp = opool.tile([P, 1], F32, name="rcp")
                 nc.vector.reciprocal(out=rcp[:], in_=small[(g, 0)][:])
                 small[(g, 1)] = rcp
-                if g == SCAST:
-                    ssteps.extend([(g, 2, now["c"] + 2), (g, 3, now["c"] + 2)])
+                if g in SCAST:
+                    ssteps.extend([(g, 2, NCN), (g, 3, NCN)])
                     done["n"] = done["n"] + 2
             elif i == 2:
                 fac = opool.tile([P, 1], F32, name="fac")
@@ -312,6 +313,8 @@ def tile_partiallyunsharedconv1d_pa_kernel(tc, x, weight, conv_bias_param, out_0
                         acc = apool.tile([P, 4 * P], F32, name="acc")
                         accs[(g, s // 2)] = acc
                     lo, hi = 0, L
+                    if c >= NARROW0 and f > 0:
+                        lo, hi = SEG_WIN[s], SEG_WIN[s] + P
                 nc.tensor.matmul_mx(
                     out=acc_slice(g, s, lo, hi),
                     lhsT=wc[:, ql * CO:(ql + 1) * CO].bitcast(FP8X4),
@@ -395,6 +398,8 @@ def tile_partiallyunsharedconv1d_pa_kernel(tc, x, weight, conv_bias_param, out_0
                     multiply(NCN + j)
             if c == dq_cycle(CPG - 1) + DLAG:
                 epilogue_scalar(DG, (0, 1, 2, 3))
+                one_scalar_step()
+                one_scalar_step()
             if c == piece_cycle(0, NPC - 1):
                 load_w(2)
                 load_d(2)
@@ -402,3 +407,5 @@ def tile_partiallyunsharedconv1d_pa_kernel(tc, x, weight, conv_bias_param, out_0
                 load_d(3)
         for i in range(len(steps) - done["n"]):
             one_step()
+        for i in range(len(ssteps) - sdone["n"]):
+            one_scalar_step()

@@ -50,7 +50,10 @@ PRE0 = 3
 SP0 = 5
 P1C0 = 5
 P1Q = (4, 6, 8, 10)
-NARROW0 = 22
+RUN_STEP = 8
+RUN_PACK = 11
+LAGT = 26
+BAR = 1024
 VS0 = 0
 
 FLOPS = 2 * G * CO * CI * KL * L
@@ -298,32 +301,83 @@ def tile_partiallyunsharedconv1d_pa_kernel(tc, x, weight, conv_bias_param, out_0
                 nc.scalar.activation(out=o8[:], in_=ress[g][:], func=ACT.Identity, scale=small[(g, 2)][:, 0:1], bias=zero[:, 0:1], saturate=False)
                 nc.sync.dma_start(out=o1_v[g], in_=o8[:].bitcast(U8))
 
-        def multiply(c):
+        pe = {"n": 0, "w": 0, "m": 0}
+        dwait = []
+        vwait = []
+
+        def one_pass(c, ql, wide):
             g, cc = divmod(c, CPG)
             wc, ws = cod[c]
-            for ql in range(QC):
-                s, f = divmod(QC * cc + ql, KL)
-                if g == DG:
-                    if f == 0 and s == 0:
-                        acc = apool.tile([P, 4 * P], F32, name="acc")
-                        accs[(g, 0)] = acc
-                    lo, hi = SEG_WIN[s], SEG_WIN[s] + P
-                else:
-                    if f == 0 and s % 2 == 0:
-                        acc = apool.tile([P, 4 * P], F32, name="acc")
-                        accs[(g, s // 2)] = acc
-                    lo, hi = 0, L
-                    if c >= NARROW0 and f > 0:
-                        lo, hi = SEG_WIN[s], SEG_WIN[s] + P
-                nc.tensor.matmul_mx(
-                    out=acc_slice(g, s, lo, hi),
-                    lhsT=wc[:, ql * CO:(ql + 1) * CO].bitcast(FP8X4),
-                    lhsT_scale=ws[:, ql * CO:(ql + 1) * CO],
-                    rhs=xsh[:, f, g, lo:hi].bitcast(FP8X4),
-                    rhs_scale=xss[4 * g:P, f, lo:hi],
-                    start=(f == 0),
-                    stop=(f == KL - 1),
-                )
+            s, f = divmod(QC * cc + ql, KL)
+            if g == DG:
+                if f == 0 and s == 0:
+                    acc = apool.tile([P, 4 * P], F32, name="acc")
+                    accs[(g, 0)] = acc
+            else:
+                if f == 0 and s % 2 == 0:
+                    acc = apool.tile([P, 4 * P], F32, name="acc")
+                    accs[(g, s // 2)] = acc
+            lo, hi = SEG_WIN[s], SEG_WIN[s] + P
+            if wide:
+                lo, hi = 0, L
+            nc.tensor.matmul_mx(
+                out=acc_slice(g, s, lo, hi),
+                lhsT=wc[:, ql * CO:(ql + 1) * CO].bitcast(FP8X4),
+                lhsT_scale=ws[:, ql * CO:(ql + 1) * CO],
+                rhs=xsh[:, f, g, lo:hi].bitcast(FP8X4),
+                rhs_scale=xss[4 * g:P, f, lo:hi],
+                start=(f == 0),
+                stop=(f == KL - 1),
+            )
+
+        def mm_run(upto, fill):
+            ms = list(range(pe["m"], upto))
+            pe["m"] = max(pe["m"], upto)
+            units = list(dwait)
+            dwait.clear()
+            wide = set([m for m in ms if m % KL == 0])
+            cols = P * (len(ms) + len(wide) + QC * len(units))
+            if fill:
+                for m in ms:
+                    if cols < BAR and m not in wide:
+                        wide.add(m)
+                        cols = cols + P
+                if cols < BAR:
+                    dummy((BAR - cols + L - 1) // L)
+            for m in ms:
+                one_pass(m // QC, m % QC, m in wide)
+                if m % NQ == NQ // 2 - 1:
+                    epilogue_scalar(m // NQ, (0, 1))
+                if m % NQ == NQ - 1:
+                    epilogue_scalar(m // NQ, (2, 3))
+                    vwait.append((m // NQ, now["c"]))
+            for u in units:
+                for ql in range(QC):
+                    one_pass(u, ql, False)
+                if u == NCYC - 1:
+                    epilogue_scalar(DG, (0, 1, 2, 3))
+                    vwait.append((DG, now["c"]))
+                    one_scalar_step()
+                    one_scalar_step()
+
+        def paired(c):
+            return PRE0 <= c < CPG or CPG + P1C0 <= c < 2 * CPG
+
+        ends = set()
+        first = {"c": 0}
+        for c in range(1, NCN + 1):
+            if c == NCN or paired(c) != paired(first["c"]):
+                n = 2 * QC * (c - first["c"])
+                k = -(-n // (RUN_PACK if paired(first["c"]) else RUN_STEP))
+                for i in range(k):
+                    ends.add(2 * QC * first["c"] + (i + 1) * n // k)
+                first["c"] = c
+
+        def after_transpose():
+            n = pe["n"] + 1
+            pe["n"] = n
+            if n in ends:
+                mm_run(min(NT * NQ, (n - LAGT) // 2 + 1), n < 2 * QC * NCN)
 
         def piece_cycle(k, u):
             return PC0[u] if k == 0 else DSTART[k] + DSTEP[k] * (u // DRATE[k])
@@ -336,6 +390,9 @@ def tile_partiallyunsharedconv1d_pa_kernel(tc, x, weight, conv_bias_param, out_0
 
         for c in range(NCN + LAGC + 2):
             now["c"] = c
+            for j in range(CPG):
+                if dq_cycle(j) + DLAG == c:
+                    dwait.append(NCN + j)
             if c < NCN:
                 g, cc = divmod(c, CPG)
                 wv = wtiles[g][:].bitcast(F32).rearrange("o (p t w) -> o t w p", t=4, w=NQ // 2)
@@ -349,11 +406,13 @@ def tile_partiallyunsharedconv1d_pa_kernel(tc, x, weight, conv_bias_param, out_0
                         for i in range(4):
                             w0 = (4 * a + i) * P
                             nc.tensor.transpose(tp[:, i * P:(i + 1) * P], prw[:, w0:w0 + P], ident[:])
+                            after_transpose()
                         src = tp[:].rearrange("p (e u o) -> p e o u", e=2, u=2)
                         dst = grouped[:, a * half:(a + 1) * half].bitcast(F32).rearrange("p (e o u) -> p e o u", e=2, u=2)
                     else:
                         for t in range(4):
                             nc.tensor.transpose(tp[:, t * P:(t + 1) * P], wv[:, t, 2 * cc + a, :], ident[:])
+                            after_transpose()
                         src = tp[:].bitcast(BF16).rearrange("p (t o e) -> p e o t", t=4, e=2)
                         dst = grouped[:, a * half:(a + 1) * half].rearrange("p (e o t) -> p e o t", e=2, t=4)
                     if a == 0 or c < VS0 or busy_with_chunks(c):
@@ -380,26 +439,12 @@ def tile_partiallyunsharedconv1d_pa_kernel(tc, x, weight, conv_bias_param, out_0
             for j in range(CPG):
                 if dq_cycle(j) == c:
                     quantise(NCN + j, 1)
-            for g in range(NT):
-                if c == (g + 1) * CPG + LAGC:
+            for g, ce in list(vwait):
+                if c > ce:
                     epilogue_vector(g)
-            if c == dq_cycle(CPG - 1) + DLAG + 1:
-                epilogue_vector(DG)
-            if c < LAGC:
-                dummy(QC)
-            elif c < NCN + LAGC:
-                multiply(c - LAGC)
-                if (c - LAGC) % CPG == CPG // 2:
-                    epilogue_scalar((c - LAGC) // CPG, (0, 1))
-                if (c - LAGC) % CPG == CPG - 1:
-                    epilogue_scalar((c - LAGC) // CPG, (2, 3))
-            for j in range(CPG):
-                if dq_cycle(j) + DLAG == c:
-                    multiply(NCN + j)
-            if c == dq_cycle(CPG - 1) + DLAG:
-                epilogue_scalar(DG, (0, 1, 2, 3))
-                one_scalar_step()
-                one_scalar_step()
+                    vwait.remove((g, ce))
+            if c >= NCN:
+                mm_run(min(NT * NQ, QC * (c - LAGC + 1)), False)
             if c == piece_cycle(0, NPC - 1):
                 load_w(2)
                 load_d(2)

from contextlib import ExitStack

import concourse.mybir as mybir
from concourse.masks import make_identity

F32 = mybir.dt.float32
BF16 = mybir.dt.bfloat16
I32 = mybir.dt.int32
U8 = mybir.dt.uint8
FP8X4 = mybir.dt.float8_e4m3fn_x4
FP8 = mybir.dt.float8_e4m3fn
ALU = mybir.AluOpType
ACT = mybir.ActivationFunctionType
AX = mybir.AxisListType
ENG = mybir.EngineType

P = 128
G = 4
CO = 128
CI = 512
NSEG = 4
KL = 9
NQ = NSEG * KL
L = 256
PAD = 4
SEG_START = (0, 58, 116, 174)
SEG_END = (58, 116, 174, 256)
SEG_WIN = (0, 0, 64, 128)
ROW = CI * NQ
QC = 4
CPG = NQ // QC
NT = 3
DG = 3
NCN = NT * CPG
NCYC = G * CPG
LAGC = 3
NWARM = 10
OCS = (24, 40, 32, 32)
OFF = (0, 24, 64, 96)
NCH = 4
DSTART = (5, 11, 20, 22)
PC0 = (5, 8, 9)
NPC = 3
DRATE = (1, 1, 2, 1)
DSTEP = (2, 2, 1, 1)
DQRATE = 3
DLAG = 2
SCAST = (1, 3)
PRE0 = 3
SP0 = 5
P1C0 = 5
P1Q = (4, 6, 8, 10)
RUN_STEP = 8
RUN_PACK = 11
LAGT = 26
BAR = 1024
VS0 = 0

FLOPS = 2 * G * CO * CI * KL * L


def tile_partiallyunsharedconv1d_pa_kernel(tc, x, weight, conv_bias_param, out_0, out_1):
    nc = tc.nc
    x_v = x.rearrange("b d k (p j) l -> p (b d k) j l", j=4)
    w_v = weight.rearrange("d k o i s u f -> (d k) o (i s u f)")
    wd_v = weight.rearrange("d k o (p t) s u f -> (d k) p o (t s u f)", t=4)
    b_v = conv_bias_param.rearrange("d k o s u -> o (d k) (s u)")
    o0_v = out_0.rearrange("b d k o l -> (b d k) o l")
    o1_v = out_1.rearrange("b d k o l -> (b d k) o l")

    with ExitStack() as ctx:
        const = ctx.enter_context(tc.tile_pool(name="const", bufs=1))
        wpool = ctx.enter_context(tc.tile_pool(name="wraw", bufs=2))
        dpool = ctx.enter_context(tc.tile_pool(name="draw", bufs=2))
        gpool = ctx.enter_context(tc.tile_pool(name="grouped", bufs=4))
        cpool = ctx.enter_context(tc.tile_pool(name="codes", bufs=LAGC + 9))
        opool = ctx.enter_context(tc.tile_pool(name="outs", bufs=3))
        spool = ctx.enter_context(tc.tile_pool(name="stage", bufs=2))
        tpool = ctx.enter_context(tc.psum_pool(name="tp", bufs=5))
        apool = ctx.enter_context(tc.psum_pool(name="acc", bufs=3))

        xraw = spool.tile([P, G, 4, L], BF16, name="stage", align_bytes=64)
        for g in range(G):
            nc.sync.dma_start(out=xraw[:, g], in_=x_v[:, g])
        biasb = const.tile([P, G, NSEG], BF16)
        nc.scalar.dma_start(out=biasb[:], in_=b_v)

        wtiles = {}
        dtiles = {}

        def load_w(g):
            wsb = wpool.tile([P, ROW], BF16, name="wsb")
            step = ROW // 4
            for c in range(4):
                nc.sync.dma_start(out=wsb[:, c * step:(c + 1) * step], in_=w_v[g, :, c * step:(c + 1) * step])
            wtiles[g] = wsb

        def load_d(k):
            dch = dpool.tile([P, max(OCS), 4 * NQ], BF16, name="dch")
            nc.sync.dma_start(out=dch[:, 0:OCS[k], :], in_=wd_v[DG, :, OFF[k]:OFF[k] + OCS[k], :])
            dtiles[k] = dch

        load_w(0)
        load_d(0)
        load_w(1)
        load_d(1)

        ident = const.tile([P, P], F32)
        make_identity(nc, ident[:])

        zero = const.tile([P, 1], F32)
        nc.vector.memset(zero[:], 0.0)
        biasf = const.tile([P, G, NSEG], F32)
        nc.vector.tensor_copy(out=biasf[:], in_=biasb[:])

        xg = spool.tile([P, G, L, 4], BF16, name="stage", align_bytes=64)
        xsh = const.tile([P, KL, G, L], I32, align_bytes=64)
        xss = const.tile([P, KL, L], U8, align_bytes=64)
        nc.vector.memset(xss[:].bitcast(I32), 0)
        nc.vector.memset(xsh[:, :, :, 0:PAD], 0)
        nc.vector.memset(xsh[:, :, :, L - PAD:L], 0)
        for g in range(G):
            src = xraw[:, g].rearrange("p j l -> p l j")
            if g % 2 == 0:
                nc.vector.tensor_copy(out=xg[:, g], in_=src)
            else:
                nc.scalar.copy(out=xg[:, g], in_=src)
        for g in range(G):
            nc.vector.quantize_mx(
                out=xsh[:, PAD, g, :].bitcast(FP8X4),
                scales=xss[4 * g:P, PAD, :],
                in_=xg[:, g].rearrange("p l j -> p (l j)"),
            )
        WID4 = QC * CO * 4
        dall = const.tile([P, CPG * WID4], BF16, align_bytes=64)
        pres = []
        for h in range((CPG - P1C0) // 2):
            pre = spool.tile([P, 2 * WID4], BF16, name="stage", align_bytes=64)
            pres.append(pre)

        def pre_ap(cc):
            return dall[:, cc * WID4:(cc + 1) * WID4]

        def pre1_ap(cc):
            j = cc - P1C0
            return pres[j // 2][:, (j % 2) * WID4:(j % 2 + 1) * WID4]

        def pair1(copy, c4, cc):
            step = ROW // 4
            q0 = QC * cc
            src = wtiles[1][:, c4 * step:(c4 + 1) * step].rearrange("o (p u e q) -> o u p e q", u=2, e=2, q=NQ)[:, :, :, :, q0:q0 + QC]
            dst = pre1_ap(cc).rearrange("o (q u p e) -> o u p e q", q=QC, u=2, e=2)[:, :, 32 * c4:32 * c4 + 32, :, :]
            copy(out=dst, in_=src)

        def pair(copy, c4, cc):
            step = ROW // 4
            q0 = QC * cc
            src = wtiles[0][:, c4 * step:(c4 + 1) * step].rearrange("o (p u e q) -> o u p e q", u=2, e=2, q=NQ)[:, :, :, :, q0:q0 + QC]
            dst = pre_ap(cc).rearrange("o (q u p e) -> o u p e q", q=QC, u=2, e=2)[:, :, 32 * c4:32 * c4 + 32, :, :]
            copy(out=dst, in_=src)

        for c4 in range(3):
            for cc in range(SP0, CPG):
                pair(nc.scalar.copy, c4, cc)

        for f in range(KL):
            d = f - PAD
            if d == 0:
                continue
            lo = max(0, -d)
            hi = min(L, L - d)
            nc.vector.tensor_copy(out=xsh[:, f, :, lo:hi], in_=xsh[:, PAD, :, lo + d:hi + d])
            nc.vector.tensor_copy(out=xss[:, f, lo:hi], in_=xss[:, PAD, lo + d:hi + d])
        for c4 in range(3):
            for cc in range(PRE0, SP0):
                pair(nc.vector.tensor_copy, c4, cc)
        for cc in range(PRE0, CPG):
            pair(nc.vector.tensor_copy, 3, cc)

        ctx.enter_context(tc.manual_schedule(engines={ENG.PE, ENG.DVE, ENG.Activation}))
        scr = apool.tile([P, 4 * P], F32, name="acc")

        def dummy(count):
            for i in range(count):
                nc.tensor.matmul_mx(
                    out=scr[:, 0:L],
                    lhsT=xsh[:, PAD, 0, 0:P].bitcast(FP8X4),
                    lhsT_scale=xss[0:P, PAD, 0:P],
                    rhs=xsh[:, PAD, 0, :].bitcast(FP8X4),
                    rhs_scale=xss[0:P, PAD, :],
                    start=True,
                    stop=True,
                )

        gate0 = 2 * (ROW // 4)
        nc.tensor.matmul(scr[:, 2 * P:3 * P], lhsT=wtiles[0][:, gate0:gate0 + P], rhs=wtiles[0][:, gate0:gate0 + P], start=True, stop=True)
        dummy(NWARM)

        gro = {}
        cod = {}
        accs = {}
        ress = {}
        small = {}

        for j in range(CPG):
            gro[NCN + j] = dall[:, j * WID4:(j + 1) * WID4]

        def regroup(k, u):
            n = min(4, CPG - 4 * u)
            src = dtiles[k][:].rearrange("p o (t j q) -> p j o t q", t=4, q=QC)[:, 4 * u:4 * u + n, 0:OCS[k], :, :]
            dst = dall[:].rearrange("p (j q o t) -> p j o t q", q=QC, o=CO, t=4)[:, 4 * u:4 * u + n, OFF[k]:OFF[k] + OCS[k], :, :]
            if k == NCH - 1 and u == NPC - 1:
                nc.scalar.copy(out=dst, in_=src)
            else:
                nc.vector.tensor_copy(out=dst, in_=src)
                one_step()

        def quantise(c, parts):
            wc = cpool.tile([P, QC * CO], I32, name="wc", align_bytes=64)
            ws = cpool.tile([P, QC * CO], U8, name="ws", align_bytes=64)
            wid = QC * CO // parts
            for k in range(parts):
                nc.vector.quantize_mx(
                    out=wc[:, k * wid:(k + 1) * wid].bitcast(FP8X4),
                    scales=ws[:, k * wid:(k + 1) * wid],
                    in_=gro[c][:, 4 * k * wid:4 * (k + 1) * wid],
                )
                one_step()
            cod[c] = (wc, ws)

        def acc_slice(g, s, lo, hi):
            if g == DG:
                base = s * P - SEG_WIN[s]
                return accs[(g, 0)][:, base + lo:base + hi]
            base = (s % 2) * L
            return accs[(g, s // 2)][:, base + lo:base + hi]

        def epilogue_scalar(g, segs):
            if segs[0] == 0:
                res = opool.tile([P, L], F32, name="res")
                ress[g] = res
            res = ress[g]
            for s in segs:
                st, en = SEG_START[s], SEG_END[s]
                nc.scalar.activation(
                    out=res[:, st:en],
                    in_=acc_slice(g, s, st, en),
                    func=ACT.Identity,
                    bias=biasf[:, g, s:s + 1],
                    scale=1.0,
                )
            if segs[-1] == NSEG - 1:
                nc.sync.dma_start(out=o0_v[g], in_=res[:])

        steps = []
        done = {"n": 0}

        def epilogue_vector(g):
            steps.extend([(g, i) for i in range(4)])

        def one_step():
            if done["n"] == len(steps):
                return
            g, i = steps[done["n"]]
            done["n"] = done["n"] + 1
            if i == 0:
                amax = opool.tile([P, 1], F32, name="amax")
                nc.vector.tensor_reduce(out=amax[:], in_=ress[g][:], axis=AX.X, op=ALU.max, apply_absolute_value=True)
                small[(g, 0)] = amax
            elif i == 1:
                rcp = opool.tile([P, 1], F32, name="rcp")
                nc.vector.reciprocal(out=rcp[:], in_=small[(g, 0)][:])
                small[(g, 1)] = rcp
                if g in SCAST:
                    ssteps.extend([(g, 2, NCN), (g, 3, NCN)])
                    done["n"] = done["n"] + 2
            elif i == 2:
                fac = opool.tile([P, 1], F32, name="fac")
                nc.vector.tensor_scalar(out=fac[:], in0=small[(g, 1)][:], scalar1=448.0, scalar2=None, op0=ALU.mult)
                small[(g, 2)] = fac
            else:
                o8 = opool.tile([P, L], FP8, name="o8")
                nc.vector.tensor_scalar(out=o8[:], in0=ress[g][:], scalar1=small[(g, 2)][:, 0:1], scalar2=None, op0=ALU.mult, saturate=False)
                nc.sync.dma_start(out=o1_v[g], in_=o8[:].bitcast(U8))

        ssteps = []
        sdone = {"n": 0}
        now = {"c": 0}

        def one_scalar_step():
            if sdone["n"] == len(ssteps) or ssteps[sdone["n"]][2] > now["c"]:
                return
            g, i, first = ssteps[sdone["n"]]
            sdone["n"] = sdone["n"] + 1
            if i == 2:
                fac = opool.tile([P, 1], F32, name="fac")
                nc.scalar.activation(out=fac[:], in_=small[(g, 1)][:], func=ACT.Identity, scale=448.0)
                small[(g, 2)] = fac
            else:
                o8 = opool.tile([P, L], FP8, name="o8")
                nc.scalar.activation(out=o8[:], in_=ress[g][:], func=ACT.Identity, scale=small[(g, 2)][:, 0:1], bias=zero[:, 0:1], saturate=False)
                nc.sync.dma_start(out=o1_v[g], in_=o8[:].bitcast(U8))

        pe = {"n": 0, "w": 0, "m": 0}
        dwait = []
        vwait = []

        def one_pass(c, ql, wide):
            g, cc = divmod(c, CPG)
            wc, ws = cod[c]
            s, f = divmod(QC * cc + ql, KL)
            if g == DG:
                if f == 0 and s == 0:
                    acc = apool.tile([P, 4 * P], F32, name="acc")
                    accs[(g, 0)] = acc
            else:
                if f == 0 and s % 2 == 0:
                    acc = apool.tile([P, 4 * P], F32, name="acc")
                    accs[(g, s // 2)] = acc
            lo, hi = SEG_WIN[s], SEG_WIN[s] + P
            if wide:
                lo, hi = 0, L
            nc.tensor.matmul_mx(
                out=acc_slice(g, s, lo, hi),
                lhsT=wc[:, ql * CO:(ql + 1) * CO].bitcast(FP8X4),
                lhsT_scale=ws[:, ql * CO:(ql + 1) * CO],
                rhs=xsh[:, f, g, lo:hi].bitcast(FP8X4),
                rhs_scale=xss[4 * g:P, f, lo:hi],
                start=(f == 0),
                stop=(f == KL - 1),
            )

        def mm_run(upto, fill):
            ms = list(range(pe["m"], upto))
            pe["m"] = max(pe["m"], upto)
            units = list(dwait)
            dwait.clear()
            wide = set([m for m in ms if m % KL == 0])
            cols = P * (len(ms) + len(wide) + QC * len(units))
            if fill:
                for m in ms:
                    if cols < BAR and m not in wide:
                        wide.add(m)
                        cols = cols + P
                if cols < BAR:
                    dummy((BAR - cols + L - 1) // L)
            for m in ms:
                one_pass(m // QC, m % QC, m in wide)
                if m % NQ == NQ // 2 - 1:
                    epilogue_scalar(m // NQ, (0, 1))
                if m % NQ == NQ - 1:
                    epilogue_scalar(m // NQ, (2, 3))
                    vwait.append((m // NQ, now["c"]))
            for u in units:
                for ql in range(QC):
                    one_pass(u, ql, False)
                if u == NCYC - 1:
                    epilogue_scalar(DG, (0, 1, 2, 3))
                    vwait.append((DG, now["c"]))
                    one_scalar_step()
                    one_scalar_step()

        def paired(c):
            return PRE0 <= c < CPG or CPG + P1C0 <= c < 2 * CPG

        ends = set()
        first = {"c": 0}
        for c in range(1, NCN + 1):
            if c == NCN or paired(c) != paired(first["c"]):
                n = 2 * QC * (c - first["c"])
                k = -(-n // (RUN_PACK if paired(first["c"]) else RUN_STEP))
                for i in range(k):
                    ends.add(2 * QC * first["c"] + (i + 1) * n // k)
                first["c"] = c

        def after_transpose():
            n = pe["n"] + 1
            pe["n"] = n
            if n in ends:
                mm_run(min(NT * NQ, (n - LAGT) // 2 + 1), n < 2 * QC * NCN)

        def piece_cycle(k, u):
            return PC0[u] if k == 0 else DSTART[k] + DSTEP[k] * (u // DRATE[k])

        def dq_cycle(j):
            return DSTART[NCH - 1] + 1 + j // DQRATE

        def busy_with_chunks(c):
            return c >= DSTART[2] or any([piece_cycle(k, u) == c for k in range(NCH) for u in range(NPC)])

        for c in range(NCN + LAGC + 2):
            now["c"] = c
            for j in range(CPG):
                if dq_cycle(j) + DLAG == c:
                    dwait.append(NCN + j)
            if c < NCN:
                g, cc = divmod(c, CPG)
                wv = wtiles[g][:].bitcast(F32).rearrange("o (p t w) -> o t w p", t=4, w=NQ // 2)
                grouped = gpool.tile([P, QC * CO * 4], BF16, name="grouped", align_bytes=64)
                gro[c] = grouped
                half = QC * CO * 2
                for a in range(2):
                    tp = tpool.tile([P, 4 * P], F32, name="tp")
                    if (g == 0 and cc >= PRE0) or (g == 1 and cc >= P1C0):
                        prw = (pre_ap(cc) if g == 0 else pre1_ap(cc)).bitcast(F32)
                        for i in range(4):
                            w0 = (4 * a + i) * P
                            nc.tensor.transpose(tp[:, i * P:(i + 1) * P], prw[:, w0:w0 + P], ident[:])
                            after_transpose()
                        src = tp[:].rearrange("p (e u o) -> p e o u", e=2, u=2)
                        dst = grouped[:, a * half:(a + 1) * half].bitcast(F32).rearrange("p (e o u) -> p e o u", e=2, u=2)
                    else:
                        for t in range(4):
                            nc.tensor.transpose(tp[:, t * P:(t + 1) * P], wv[:, t, 2 * cc + a, :], ident[:])
                            after_transpose()
                        src = tp[:].bitcast(BF16).rearrange("p (t o e) -> p e o t", t=4, e=2)
                        dst = grouped[:, a * half:(a + 1) * half].rearrange("p (e o t) -> p e o t", e=2, t=4)
                    if a == 0 or c < VS0 or busy_with_chunks(c):
                        nc.scalar.copy(out=dst, in_=src)
                        one_scalar_step()
                    else:
                        nc.vector.tensor_copy(out=dst, in_=src)
                        one_step()
            for c4 in range(4):
                for k in range(CPG - P1C0):
                    if P1Q[c4] + k // 2 == c and k % 2 == 0:
                        pair1(nc.scalar.copy, c4, P1C0 + k)
            if 1 <= c <= NCN:
                quantise(c - 1, 2 if c == NCN else 1)
            for c4 in range(4):
                for k in range(CPG - P1C0):
                    if P1Q[c4] + k // 2 == c and k % 2 == 1:
                        pair1(nc.vector.tensor_copy, c4, P1C0 + k)
                        one_step()
            for k in range(NCH):
                for u in range(NPC):
                    if piece_cycle(k, u) == c:
                        regroup(k, u)
            for j in range(CPG):
                if dq_cycle(j) == c:
                    quantise(NCN + j, 1)
            for g, ce in list(vwait):
                if c > ce:
                    epilogue_vector(g)
                    vwait.remove((g, ce))
            if c >= NCN:
                mm_run(min(NT * NQ, QC * (c - LAGC + 1)), False)
            if c == piece_cycle(0, NPC - 1):
                load_w(2)
                load_d(2)
            if c == piece_cycle(1, NPC - 1):
                load_d(3)
        for i in range(len(steps) - done["n"]):
            one_step()
        for i in range(len(ssteps) - sdone["n"]):
            one_scalar_step()
